import numpy as np
import ml_dtypes


def mxq(x, axis, fmt="e4m3"):
    dtype, down = {"e4m3": (ml_dtypes.float8_e4m3fn, 7), "e5m2": (ml_dtypes.float8_e5m2, 14)}[fmt]
    v = np.moveaxis(np.asarray(x, np.float32).astype(ml_dtypes.bfloat16).astype(np.float64), axis, -1)
    blocks = v.reshape(v.shape[:-1] + (-1, 32))
    amax = np.abs(blocks).max(-1, keepdims=True)
    byte = np.maximum(np.where(amax > 0, np.frexp(amax)[1] - 1 + 127, 0) - down, 1)
    scale = np.exp2(byte - 127.0)
    codes = (blocks / scale).astype(np.float32).astype(dtype).astype(np.float64)
    return np.moveaxis((codes * scale).reshape(v.shape), -1, axis)


WIDE = False


def mx_kscale(k):
    if not WIDE:
        return np.ones(k)
    levels = np.array([10, -10, 5, -5, 0])
    a = np.random.permutation(np.resize(levels, k // 512 * 4)).reshape(k // 512, 4)
    idx = np.arange(k)
    return np.exp2(a[idx // 512, idx % 128 // 32])


BF16 = ml_dtypes.bfloat16


def bf(x):
    return np.asarray(x, np.float32).astype(BF16)


def f64(x):
    return np.asarray(x).astype(np.float64)


E2M1 = np.array([0.0, 0.5, 1.0, 1.5, 2.0, 3.0, 4.0, 6.0, -0.0, -0.5, -1.0, -1.5, -2.0, -3.0, -4.0, -6.0])


def pack_weight(w, fmt):
    k, n = w.shape
    w = f64(bf(w)).reshape(k // 32, 32, n)
    amax = np.abs(w).max(1)
    if fmt == "e4m3":
        byte = np.frexp(amax)[1] - 1 + 127 - 7
    else:
        mant, ex = np.frexp(amax / 6.0)
        byte = np.where(mant > 0.5, ex, ex - 1) + 127
    byte = np.clip(np.where(amax > 0, byte, 1), 1, 254)
    scaled = (w * np.exp2(127.0 - byte)[:, None, :]).reshape(k, n).astype(np.float32)
    by_word = np.ascontiguousarray(scaled.reshape(k // 512, 128, 4, n).transpose(0, 1, 3, 2))
    if fmt == "e4m3":
        words = by_word.astype(ml_dtypes.float8_e4m3fn).view(np.uint8)
    else:
        c = by_word.astype(ml_dtypes.float4_e2m1fn).view(np.uint8) & 0xF
        words = c[..., 0::2] | (c[..., 1::2] << 4)
    return np.ascontiguousarray(words), np.ascontiguousarray(byte.astype(np.uint8).reshape(k // 512, 16, n))


def unpack_weight(words, scales, fmt):
    g, p, n, _ = words.shape
    if fmt == "e4m3":
        vals = np.ascontiguousarray(words).view(ml_dtypes.float8_e4m3fn).astype(np.float64)
    else:
        nib = np.empty((g, p, n, 4), np.uint8)
        nib[..., 0::2] = words & 0xF
        nib[..., 1::2] = words >> 4
        vals = E2M1[nib]
    vals = vals * np.repeat(np.exp2(scales.astype(np.float64) - 127.0), 8, axis=1)[..., None]
    return vals.transpose(0, 1, 3, 2).reshape(g * 512, n)

def pack4(w):
    words, scales = pack_weight(w, "e2m1")
    return words.reshape(words.shape[0], 128, -1), scales


def unpack4(words, scales):
    return unpack_weight(words.reshape(words.shape[0], 128, -1, 2), scales, "e2m1")


B, L, D, H, DH = 2, 64, 8192, 16, 64
THETA = 100000.0
E = H * DH


def rope(t):
    pos = np.arange(L, dtype=np.float64)
    inv_freq = 1.0 / THETA ** (np.arange(0, DH, 2, dtype=np.float64) / DH)
    ang = pos[:, None] * inv_freq[None, :]
    cos = np.cos(ang)[:, :, None]
    sin = np.sin(ang)[:, :, None]
    tp = t.reshape(*t.shape[:-1], DH // 2, 2)
    x1, x2 = tp[..., 0], tp[..., 1]
    rot = np.stack([-x2, x1], axis=-1)
    out = tp * cos + rot * sin
    return out.reshape(*t.shape)


def setup_inputs():
    s = mx_kscale(D)
    x = bf(np.random.standard_normal((B, L, D)) * s)
    w = np.random.standard_normal((3 * E, D)) / np.sqrt(D) / s
    words, scales = pack4(np.ascontiguousarray(w.T))
    return {"x": x, "W_words": words, "W_scales": scales}


def reference(x, W_words, W_scales):
    qkv = mxq(f64(x), 2, "e4m3") @ unpack4(W_words, W_scales)
    qkv = qkv.reshape(B, L, 3, H, DH)
    qkv = np.transpose(qkv, (0, 3, 1, 2, 4))
    q, k, v = qkv[..., 0, :], qkv[..., 1, :], qkv[..., 2, :]
    return rope(q), rope(k), np.ascontiguousarray(v)

@@ -1,0 +1,180 @@
+import math
+from contextlib import ExitStack
+
+import concourse.mybir as mybir
+from concourse.masks import make_identity
+
+F32 = mybir.dt.float32
+BF16 = mybir.dt.bfloat16
+I32 = mybir.dt.int32
+U32 = mybir.dt.uint32
+U8 = mybir.dt.uint8
+FP8X4 = mybir.dt.float8_e4m3fn_x4
+FP4X4 = mybir.dt.float4_e2m1fn_x4
+ALU = mybir.AluOpType
+ACT = mybir.ActivationFunctionType
+
+P = 128
+PACK = 4
+K_PASS = P * PACK
+BATCH, POSITIONS, D_MODEL, HEADS, HEAD_DIM = 2, 64, 8192, 16, 64
+PAIRS = HEAD_DIM // 2
+THETA = 100000.0
+SECTION = HEADS * HEAD_DIM
+N_OUT = 3 * SECTION
+PASSES = D_MODEL // K_PASS
+BANK = 512
+BANKS = N_OUT // BANK
+BANK_HEADS = BANK // HEAD_DIM
+X_CHUNK_PASSES = 4
+ROUND_PASSES = 2
+SCALE_DMA_PASSES = 8
+ROUND_TO_INTEGER = 1.5 * 2.0**23
+
+FLOPS = 2 * P * D_MODEL * N_OUT
+
+
+def tile_multiheadselfattention_pa_k_kernel(tc, x, W_words, W_scales, out_0, out_1, out_2):
+    nc = tc.nc
+    with ExitStack() as ctx:
+        ctx.enter_context(tc.manual_schedule())
+        keep = ctx.enter_context(tc.tile_pool(name="keep", bufs=1))
+        x_pool = ctx.enter_context(tc.tile_pool(name="x", bufs=PASSES // X_CHUNK_PASSES))
+        group_pool = ctx.enter_context(tc.tile_pool(name="group", bufs=3))
+        rope_pool = ctx.enter_context(tc.tile_pool(name="rope", bufs=2))
+        psum_t = ctx.enter_context(tc.psum_pool(name="psum_t", bufs=2))
+        psum_acc = ctx.enter_context(tc.psum_pool(name="psum_acc", bufs=1))
+
+        w_words = keep.tile([P, PASSES, 2 * N_OUT], U8, align_bytes=64)
+        w_scales = keep.tile([P, PASSES, N_OUT], U8, align_bytes=64)
+        x_codes = keep.tile([P, PASSES, P], U32, align_bytes=64)
+        x_scales = keep.tile([P, PASSES, P], U8, align_bytes=64)
+        ident = keep.tile([P, P], F32)
+        make_identity(nc, ident[:])
+
+        x_rows = x.rearrange("b l c -> l b c")
+        x_cols = X_CHUNK_PASSES * K_PASS
+        x_chunks = []
+        for c in range(PASSES // X_CHUNK_PASSES):
+            x_sb = x_pool.tile([P, x_cols], BF16)
+            nc.sync.dma_start(out=x_sb[:], in_=x_rows[:, :, c * x_cols : (c + 1) * x_cols])
+            x_chunks.append(x_sb)
+
+        scale_rows = W_scales.bitcast(I32).rearrange("g q n -> q g n")
+        for g0 in range(0, PASSES, SCALE_DMA_PASSES):
+            g1 = g0 + SCALE_DMA_PASSES
+            nc.vector.memset(w_scales[:, g0:g1, :].bitcast(I32), 0)
+            for b in range(2):
+                for r in range(4):
+                    nc.sync.dma_start(
+                        out=w_scales[32 * b + r : P : 64, g0:g1, :].bitcast(I32),
+                        in_=scale_rows[4 * b + r : 16 : 8, g0:g1, :],
+                    )
+
+        for g in range(PASSES):
+            nc.sync.dma_start(out=w_words[:, g, :].bitcast(I32), in_=W_words[g].bitcast(I32))
+
+        for j in range(PASSES // ROUND_PASSES):
+            xt = psum_t.tile([P, ROUND_PASSES, 2, P], F32)
+            for gi in range(ROUND_PASSES):
+                g = ROUND_PASSES * j + gi
+                words = x_chunks[g // X_CHUNK_PASSES][:].bitcast(F32)
+                first = (g % X_CHUNK_PASSES) * (K_PASS // 2)
+                for u in range(2):
+                    nc.tensor.transpose(
+                        xt[:, gi, u, :], words[:, first + u : first + K_PASS // 2 : 2], ident[:]
+                    )
+            grouped = group_pool.tile([P, ROUND_PASSES, P, PACK], BF16, align_bytes=64)
+            nc.scalar.copy(out=grouped[:].bitcast(F32), in_=xt[:].rearrange("p g u r -> p g r u"))
+            g0 = ROUND_PASSES * j
+            g1 = g0 + ROUND_PASSES
+            nc.vector.quantize_mx(
+                out=x_codes[:, g0:g1, :].rearrange("p g r -> p (g r)").bitcast(FP8X4),
+                scales=x_scales[:, g0:g1, :].rearrange("p g r -> p (g r)"),
+                in_=grouped[:].rearrange("p g r t -> p (g r t)"),
+            )
+
+        partition_index = keep.tile([P, 1], I32)
+        nc.gpsimd.iota(out=partition_index[:], pattern=[[0, 1]], base=0, channel_multiplier=1)
+        pair_index = keep.tile([P, PAIRS], I32)
+        nc.gpsimd.iota(out=pair_index[:], pattern=[[1, PAIRS]], base=0, channel_multiplier=0)
+        position_index = keep.tile([P, 1], I32)
+        nc.vector.tensor_single_scalar(
+            out=position_index[:], in_=partition_index[:], scalar=1, op=ALU.arith_shift_right
+        )
+        position = keep.tile([P, 1], F32)
+        nc.vector.tensor_copy(out=position[:], in_=position_index[:])
+        pair = keep.tile([P, PAIRS], F32)
+        nc.vector.tensor_copy(out=pair[:], in_=pair_index[:])
+        inv_freq = keep.tile([P, PAIRS], F32)
+        nc.scalar.activation(out=inv_freq[:], in_=pair[:], func=ACT.Exp, scale=-math.log(THETA) / PAIRS)
+        turns = keep.tile([P, 2, PAIRS], F32)
+        nc.vector.tensor_scalar(
+            out=turns[:, 1, :],
+            in0=inv_freq[:],
+            scalar1=position[:, 0:1],
+            scalar2=1.0 / (2.0 * math.pi),
+            op0=ALU.mult,
+            op1=ALU.mult,
+        )
+        nc.vector.tensor_scalar_add(out=turns[:, 0, :], in0=turns[:, 1, :], scalar1=0.25)
+        shifted = keep.tile([P, 2, PAIRS], F32)
+        nc.vector.tensor_scalar_add(out=shifted[:], in0=turns[:], scalar1=ROUND_TO_INTEGER)
+        whole = keep.tile([P, 2, PAIRS], F32)
+        nc.vector.tensor_scalar_sub(out=whole[:], in0=shifted[:], scalar1=ROUND_TO_INTEGER)
+        fraction = keep.tile([P, 2, PAIRS], F32)
+        nc.vector.tensor_sub(out=fraction[:], in0=turns[:], in1=whole[:])
+        cos_sin = keep.tile([P, 2, PAIRS], F32)
+        nc.scalar.activation(out=cos_sin[:], in_=fraction[:], func=ACT.Sin, scale=2.0 * math.pi)
+        neg_sin = keep.tile([P, PAIRS], F32)
+        nc.vector.tensor_scalar_mul(out=neg_sin[:], in0=cos_sin[:, 1, :], scalar1=-1.0)
+
+        def over_heads(table, planes):
+            return table.unsqueeze(1).unsqueeze(1).to_broadcast([P, planes, BANK_HEADS, PAIRS])
+
+        acc = [psum_acc.tile([P, BANK], F32, name="acc%d" % n) for n in range(BANKS)]
+        for g in range(PASSES):
+            for n in range(BANKS):
+                nc.tensor.matmul_mx(
+                    out=acc[n][:],
+                    lhsT=x_codes[:, g, :].bitcast(FP8X4),
+                    lhsT_scale=x_scales[:, g, :],
+                    rhs=w_words[:, g, 2 * BANK * n : 2 * BANK * (n + 1)].bitcast(FP4X4),
+                    rhs_scale=w_scales[:, g, BANK * n : BANK * (n + 1)],
+                    start=(g == 0),
+                    stop=(g == PASSES - 1),
+                )
+
+        for section, out in enumerate((out_0, out_1, out_2)):
+            result = keep.tile([P, HEADS, PAIRS, 2], F32, name="result%d" % section)
+            for half in range(2):
+                bank = acc[2 * section + half]
+                heads = slice(BANK_HEADS * half, BANK_HEADS * (half + 1))
+                if section == 2:
+                    nc.scalar.copy(
+                        out=result[:, heads, :, :],
+                        in_=bank[:].rearrange("p (h i e) -> p h i e", i=PAIRS, e=2),
+                    )
+                    continue
+                by_plane = bank[:].rearrange("p (h i e) -> p e h i", i=PAIRS, e=2)
+                with_cos = rope_pool.tile([P, 2, BANK_HEADS, PAIRS], F32)
+                nc.vector.tensor_tensor(
+                    out=with_cos[:], in0=by_plane, in1=over_heads(cos_sin[:, 0, :], 2), op=ALU.mult
+                )
+                with_sin = rope_pool.tile([P, 2, BANK_HEADS, PAIRS], F32)
+                nc.vector.tensor_tensor(
+                    out=with_sin[:, 0:1, :, :], in0=by_plane[:, 1:2, :, :], in1=over_heads(neg_sin[:], 1), op=ALU.mult
+                )
+                nc.vector.tensor_tensor(
+                    out=with_sin[:, 1:2, :, :], in0=by_plane[:, 0:1, :, :], in1=over_heads(cos_sin[:, 1, :], 1), op=ALU.mult
+                )
+                nc.gpsimd.tensor_tensor(
+                    out=result[:, heads, :, :],
+                    in0=with_cos[:].rearrange("p e h i -> p h i e"),
+                    in1=with_sin[:].rearrange("p e h i -> p h i e"),
+                    op=ALU.add,
+                )
+            nc.sync.dma_start(
+                out=out.rearrange("b h l d -> l b h d"),
+                in_=result[:].rearrange("p h i e -> p h (i e)"),
+            )

@@ -28,7 +28,6 @@ BANKS = N_OUT // BANK
 BANK_HEADS = BANK // HEAD_DIM
 X_CHUNK_PASSES = 4
 ROUND_PASSES = 2
-SCALE_DMA_PASSES = 8
 ROUND_TO_INTEGER = 1.5 * 2.0**23
 
 FLOPS = 2 * P * D_MODEL * N_OUT
@@ -61,15 +60,12 @@ def tile_multiheadselfattention_pa_k_kernel(tc, x, W_words, W_scales, out_0, out
             x_chunks.append(x_sb)
 
         scale_rows = W_scales.bitcast(I32).rearrange("g q n -> q g n")
-        for g0 in range(0, PASSES, SCALE_DMA_PASSES):
-            g1 = g0 + SCALE_DMA_PASSES
-            nc.vector.memset(w_scales[:, g0:g1, :].bitcast(I32), 0)
-            for b in range(2):
-                for r in range(4):
-                    nc.sync.dma_start(
-                        out=w_scales[32 * b + r : P : 64, g0:g1, :].bitcast(I32),
-                        in_=scale_rows[4 * b + r : 16 : 8, g0:g1, :],
-                    )
+        nc.vector.memset(w_scales[:].bitcast(I32), 0)
+        for quadrant in range(4):
+            for r in range(4):
+                q = 4 * quadrant + r
+                p = 32 * quadrant + r
+                nc.sync.dma_start(out=w_scales[p : p + 1, :, :].bitcast(I32), in_=scale_rows[q : q + 1, :, :])
 
         for g in range(PASSES):
             nc.sync.dma_start(out=w_words[:, g, :].bitcast(I32), in_=W_words[g].bitcast(I32))

@@ -28,6 +28,10 @@ BANKS = N_OUT // BANK
 BANK_HEADS = BANK // HEAD_DIM
 X_CHUNK_PASSES = 4
 ROUND_PASSES = 2
+SCALE_DMA_PASSES = 8
+TAIL_PASSES = 4
+MAIN_PASSES = PASSES - TAIL_PASSES
+TAIL_DMA_PASSES = 2
 ROUND_TO_INTEGER = 1.5 * 2.0**23
 
 FLOPS = 2 * P * D_MODEL * N_OUT
@@ -60,15 +64,26 @@ def tile_multiheadselfattention_pa_k_kernel(tc, x, W_words, W_scales, out_0, out
             x_chunks.append(x_sb)
 
         scale_rows = W_scales.bitcast(I32).rearrange("g q n -> q g n")
-        nc.vector.memset(w_scales[:].bitcast(I32), 0)
-        for quadrant in range(4):
-            for r in range(4):
-                q = 4 * quadrant + r
-                p = 32 * quadrant + r
-                nc.sync.dma_start(out=w_scales[p : p + 1, :, :].bitcast(I32), in_=scale_rows[q : q + 1, :, :])
+        for g0 in range(0, PASSES, SCALE_DMA_PASSES):
+            g1 = g0 + SCALE_DMA_PASSES
+            nc.vector.memset(w_scales[:, g0:g1, :].bitcast(I32), 0)
+            for b in range(2):
+                for r in range(4):
+                    nc.sync.dma_start(
+                        out=w_scales[32 * b + r : P : 64, g0:g1, :].bitcast(I32),
+                        in_=scale_rows[4 * b + r : 16 : 8, g0:g1, :],
+                    )
 
-        for g in range(PASSES):
+        for g in range(MAIN_PASSES):
             nc.sync.dma_start(out=w_words[:, g, :].bitcast(I32), in_=W_words[g].bitcast(I32))
+        word_rows = W_words.bitcast(I32).rearrange("g p n -> p g n")
+        for section in range(3):
+            for g0 in range(MAIN_PASSES, PASSES, TAIL_DMA_PASSES):
+                g1 = g0 + TAIL_DMA_PASSES
+                nc.sync.dma_start(
+                    out=w_words[:, g0:g1, 2 * SECTION * section : 2 * SECTION * (section + 1)].bitcast(I32),
+                    in_=word_rows[:, g0:g1, SECTION // 2 * section : SECTION // 2 * (section + 1)],
+                )
 
         for j in range(PASSES // ROUND_PASSES):
             xt = psum_t.tile([P, ROUND_PASSES, 2, P], F32)
@@ -129,19 +144,26 @@ def tile_multiheadselfattention_pa_k_kernel(tc, x, W_words, W_scales, out_0, out
             return table.unsqueeze(1).unsqueeze(1).to_broadcast([P, planes, BANK_HEADS, PAIRS])
 
         acc = [psum_acc.tile([P, BANK], F32, name="acc%d" % n) for n in range(BANKS)]
-        for g in range(PASSES):
+
+        def mx_pass(g, n):
+            nc.tensor.matmul_mx(
+                out=acc[n][:],
+                lhsT=x_codes[:, g, :].bitcast(FP8X4),
+                lhsT_scale=x_scales[:, g, :],
+                rhs=w_words[:, g, 2 * BANK * n : 2 * BANK * (n + 1)].bitcast(FP4X4),
+                rhs_scale=w_scales[:, g, BANK * n : BANK * (n + 1)],
+                start=(g == 0),
+                stop=(g == PASSES - 1),
+            )
+
+        for g in range(MAIN_PASSES):
             for n in range(BANKS):
-                nc.tensor.matmul_mx(
-                    out=acc[n][:],
-                    lhsT=x_codes[:, g, :].bitcast(FP8X4),
-                    lhsT_scale=x_scales[:, g, :],
-                    rhs=w_words[:, g, 2 * BANK * n : 2 * BANK * (n + 1)].bitcast(FP4X4),
-                    rhs_scale=w_scales[:, g, BANK * n : BANK * (n + 1)],
-                    start=(g == 0),
-                    stop=(g == PASSES - 1),
-                )
+                mx_pass(g, n)
 
         for section, out in enumerate((out_0, out_1, out_2)):
+            for g in range(MAIN_PASSES, PASSES):
+                for half in range(2):
+                    mx_pass(g, 2 * section + half)
             result = keep.tile([P, HEADS, PAIRS, 2], F32, name="result%d" % section)
             for half in range(2):
                 bank = acc[2 * section + half]

@@ -48,7 +48,8 @@ def tile_multiheadselfattention_pa_k_kernel(tc, x, W_words, W_scales, out_0, out
         psum_t = ctx.enter_context(tc.psum_pool(name="psum_t", bufs=2))
         psum_acc = ctx.enter_context(tc.psum_pool(name="psum_acc", bufs=1))
 
-        w_words = keep.tile([P, PASSES, 2 * N_OUT], U8, align_bytes=64)
+        w_words = keep.tile([P, MAIN_PASSES, 2 * N_OUT], U8, align_bytes=64)
+        w_tail = [keep.tile([P, TAIL_PASSES, 2 * SECTION], U8, align_bytes=64, name="w_tail%d" % s) for s in range(3)]
         w_scales = keep.tile([P, PASSES, N_OUT], U8, align_bytes=64)
         x_codes = keep.tile([P, PASSES, P], U32, align_bytes=64)
         x_scales = keep.tile([P, PASSES, P], U8, align_bytes=64)
@@ -78,11 +79,13 @@ def tile_multiheadselfattention_pa_k_kernel(tc, x, W_words, W_scales, out_0, out
             nc.sync.dma_start(out=w_words[:, g, :].bitcast(I32), in_=W_words[g].bitcast(I32))
         word_rows = W_words.bitcast(I32).rearrange("g p n -> p g n")
         for section in range(3):
-            for g0 in range(MAIN_PASSES, PASSES, TAIL_DMA_PASSES):
-                g1 = g0 + TAIL_DMA_PASSES
+            for t0 in range(0, TAIL_PASSES, TAIL_DMA_PASSES):
+                t1 = t0 + TAIL_DMA_PASSES
                 nc.sync.dma_start(
-                    out=w_words[:, g0:g1, 2 * SECTION * section : 2 * SECTION * (section + 1)].bitcast(I32),
-                    in_=word_rows[:, g0:g1, SECTION // 2 * section : SECTION // 2 * (section + 1)],
+                    out=w_tail[section][:, t0:t1, :].bitcast(I32),
+                    in_=word_rows[
+                        :, MAIN_PASSES + t0 : MAIN_PASSES + t1, SECTION // 2 * section : SECTION // 2 * (section + 1)
+                    ],
                 )
 
         for j in range(PASSES // ROUND_PASSES):
@@ -145,12 +148,12 @@ def tile_multiheadselfattention_pa_k_kernel(tc, x, W_words, W_scales, out_0, out
 
         acc = [psum_acc.tile([P, BANK], F32, name="acc%d" % n) for n in range(BANKS)]
 
-        def mx_pass(g, n):
+        def mx_pass(g, n, words):
             nc.tensor.matmul_mx(
                 out=acc[n][:],
                 lhsT=x_codes[:, g, :].bitcast(FP8X4),
                 lhsT_scale=x_scales[:, g, :],
-                rhs=w_words[:, g, 2 * BANK * n : 2 * BANK * (n + 1)].bitcast(FP4X4),
+                rhs=words.bitcast(FP4X4),
                 rhs_scale=w_scales[:, g, BANK * n : BANK * (n + 1)],
                 start=(g == 0),
                 stop=(g == PASSES - 1),
@@ -158,12 +161,14 @@ def tile_multiheadselfattention_pa_k_kernel(tc, x, W_words, W_scales, out_0, out
 
         for g in range(MAIN_PASSES):
             for n in range(BANKS):
-                mx_pass(g, n)
+                mx_pass(g, n, w_words[:, g, 2 * BANK * n : 2 * BANK * (n + 1)])
 
         for section, out in enumerate((out_0, out_1, out_2)):
-            for g in range(MAIN_PASSES, PASSES):
+            for t in range(TAIL_PASSES):
                 for half in range(2):
-                    mx_pass(g, 2 * section + half)
+                    mx_pass(
+                        MAIN_PASSES + t, 2 * section + half, w_tail[section][:, t, 2 * BANK * half : 2 * BANK * (half + 1)]
+                    )
             result = keep.tile([P, HEADS, PAIRS, 2], F32, name="result%d" % section)
             for half in range(2):
                 bank = acc[2 * section + half]

@@ -29,6 +29,7 @@ BANK_HEADS = BANK // HEAD_DIM
 X_CHUNK_PASSES = 4
 ROUND_PASSES = 2
 SCALE_DMA_PASSES = 8
+SCALE_DMAS_AHEAD = 2
 TAIL_PASSES = 4
 MAIN_PASSES = PASSES - TAIL_PASSES
 TAIL_DMA_PASSES = 2
@@ -74,19 +75,6 @@ def tile_multiheadselfattention_pa_k_kernel(tc, x, W_words, W_scales, out_0, out
                         out=w_scales[32 * b + r : P : 64, g0:g1, :].bitcast(I32),
                         in_=scale_rows[4 * b + r : 16 : 8, g0:g1, :],
                     )
-
-        for g in range(MAIN_PASSES):
-            nc.sync.dma_start(out=w_words[:, g, :].bitcast(I32), in_=W_words[g].bitcast(I32))
-        word_rows = W_words.bitcast(I32).rearrange("g p n -> p g n")
-        for section in range(3):
-            for t0 in range(0, TAIL_PASSES, TAIL_DMA_PASSES):
-                t1 = t0 + TAIL_DMA_PASSES
-                nc.sync.dma_start(
-                    out=w_tail[section][:, t0:t1, :].bitcast(I32),
-                    in_=word_rows[
-                        :, MAIN_PASSES + t0 : MAIN_PASSES + t1, SECTION // 2 * section : SECTION // 2 * (section + 1)
-                    ],
-                )
 
         for j in range(PASSES // ROUND_PASSES):
             xt = psum_t.tile([P, ROUND_PASSES, 2, P], F32)
@@ -142,6 +130,23 @@ def tile_multiheadselfattention_pa_k_kernel(tc, x, W_words, W_scales, out_0, out
         nc.scalar.activation(out=cos_sin[:], in_=fraction[:], func=ACT.Sin, scale=2.0 * math.pi)
         neg_sin = keep.tile([P, PAIRS], F32)
         nc.vector.tensor_scalar_mul(out=neg_sin[:], in0=cos_sin[:, 1, :], scalar1=-1.0)
+
+        held_for = slice(32, 32 + 4 - SCALE_DMAS_AHEAD)
+        nc.vector.tensor_copy(
+            out=w_words[held_for, 0, 0:4].bitcast(I32), in_=w_scales[held_for, PASSES - 1, 0:4].bitcast(I32)
+        )
+        for g in range(MAIN_PASSES):
+            nc.sync.dma_start(out=w_words[:, g, :].bitcast(I32), in_=W_words[g].bitcast(I32))
+        word_rows = W_words.bitcast(I32).rearrange("g p n -> p g n")
+        for section in range(3):
+            for t0 in range(0, TAIL_PASSES, TAIL_DMA_PASSES):
+                t1 = t0 + TAIL_DMA_PASSES
+                nc.sync.dma_start(
+                    out=w_tail[section][:, t0:t1, :].bitcast(I32),
+                    in_=word_rows[
+                        :, MAIN_PASSES + t0 : MAIN_PASSES + t1, SECTION // 2 * section : SECTION // 2 * (section + 1)
+                    ],
+                )
 
         def over_heads(table, planes):
             return table.unsqueeze(1).unsqueeze(1).to_broadcast([P, planes, BANK_HEADS, PAIRS])

@@ -30,7 +30,7 @@ X_CHUNK_PASSES = 4
 ROUND_PASSES = 2
 SCALE_DMA_PASSES = 8
 SCALE_DMAS_AHEAD = 2
-TAIL_PASSES = 4
+TAIL_PASSES = 8
 MAIN_PASSES = PASSES - TAIL_PASSES
 TAIL_DMA_PASSES = 2
 ROUND_TO_INTEGER = 1.5 * 2.0**23

@@ -29,7 +29,7 @@ BANK_HEADS = BANK // HEAD_DIM
 X_CHUNK_PASSES = 4
 ROUND_PASSES = 2
 SCALE_DMA_PASSES = 8
-SCALE_DMAS_AHEAD = 2
+SCALE_DMAS_AHEAD = 4
 TAIL_PASSES = 8
 MAIN_PASSES = PASSES - TAIL_PASSES
 TAIL_DMA_PASSES = 2
@@ -96,6 +96,11 @@ def tile_multiheadselfattention_pa_k_kernel(tc, x, W_words, W_scales, out_0, out
                 in_=grouped[:].rearrange("p g r t -> p (g r t)"),
             )
 
+        held_for = slice(0, 8 - SCALE_DMAS_AHEAD) if SCALE_DMAS_AHEAD >= 4 else slice(32, 32 + 4 - SCALE_DMAS_AHEAD)
+        nc.vector.tensor_copy(
+            out=w_words[held_for, 0, 0:4].bitcast(I32), in_=w_scales[held_for, PASSES - 1, 0:4].bitcast(I32)
+        )
+
         partition_index = keep.tile([P, 1], I32)
         nc.gpsimd.iota(out=partition_index[:], pattern=[[0, 1]], base=0, channel_multiplier=1)
         pair_index = keep.tile([P, PAIRS], I32)
@@ -131,10 +136,6 @@ def tile_multiheadselfattention_pa_k_kernel(tc, x, W_words, W_scales, out_0, out
         neg_sin = keep.tile([P, PAIRS], F32)
         nc.vector.tensor_scalar_mul(out=neg_sin[:], in0=cos_sin[:, 1, :], scalar1=-1.0)
 
-        held_for = slice(32, 32 + 4 - SCALE_DMAS_AHEAD)
-        nc.vector.tensor_copy(
-            out=w_words[held_for, 0, 0:4].bitcast(I32), in_=w_scales[held_for, PASSES - 1, 0:4].bitcast(I32)
-        )
         for g in range(MAIN_PASSES):
             nc.sync.dma_start(out=w_words[:, g, :].bitcast(I32), in_=W_words[g].bitcast(I32))
         word_rows = W_words.bitcast(I32).rearrange("g p n -> p g n")

@@ -140,8 +140,10 @@ def tile_multiheadselfattention_pa_k_kernel(tc, x, W_words, W_scales, out_0, out
             nc.sync.dma_start(out=w_words[:, g, :].bitcast(I32), in_=W_words[g].bitcast(I32))
         word_rows = W_words.bitcast(I32).rearrange("g p n -> p g n")
         for section in range(3):
-            for t0 in range(0, TAIL_PASSES, TAIL_DMA_PASSES):
-                t1 = t0 + TAIL_DMA_PASSES
+            starts = list(range(0, TAIL_PASSES, TAIL_DMA_PASSES))
+            if section == 2:
+                starts.append(TAIL_PASSES - 1)
+            for t0, t1 in zip(starts, starts[1:] + [TAIL_PASSES]):
                 nc.sync.dma_start(
                     out=w_tail[section][:, t0:t1, :].bitcast(I32),
                     in_=word_rows[
@@ -180,10 +182,17 @@ def tile_multiheadselfattention_pa_k_kernel(tc, x, W_words, W_scales, out_0, out
                 bank = acc[2 * section + half]
                 heads = slice(BANK_HEADS * half, BANK_HEADS * (half + 1))
                 if section == 2:
-                    nc.scalar.copy(
+                    copy = nc.scalar.copy if half == 0 else nc.vector.tensor_copy
+                    copy(
                         out=result[:, heads, :, :],
                         in_=bank[:].rearrange("p (h i e) -> p h i e", i=PAIRS, e=2),
                     )
+                    queue = nc.scalar if half == 0 else nc.sync
+                    for b in range(BATCH):
+                        queue.dma_start(
+                            out=out[b, heads, :, :].rearrange("h l d -> l h d"),
+                            in_=result[b:P:BATCH, heads, :, :].rearrange("p h i e -> p h (i e)"),
+                        )
                     continue
                 by_plane = bank[:].rearrange("p (h i e) -> p e h i", i=PAIRS, e=2)
                 with_cos = rope_pool.tile([P, 2, BANK_HEADS, PAIRS], F32)
@@ -203,7 +212,8 @@ def tile_multiheadselfattention_pa_k_kernel(tc, x, W_words, W_scales, out_0, out
                     in1=with_sin[:].rearrange("p e h i -> p h i e"),
                     op=ALU.add,
                 )
-            nc.sync.dma_start(
-                out=out.rearrange("b h l d -> l b h d"),
-                in_=result[:].rearrange("p h i e -> p h (i e)"),
-            )
+            if section < 2:
+                nc.sync.dma_start(
+                    out=out.rearrange("b h l d -> l b h d"),
+                    in_=result[:].rearrange("p h i e -> p h (i e)"),
+                )

@@ -30,9 +30,8 @@ X_CHUNK_PASSES = 4
 ROUND_PASSES = 2
 SCALE_DMA_PASSES = 8
 SCALE_DMAS_AHEAD = 4
-TAIL_PASSES = 8
-MAIN_PASSES = PASSES - TAIL_PASSES
-TAIL_DMA_PASSES = 2
+QK_BANKS = 4
+V_DMA_PASSES = 2
 ROUND_TO_INTEGER = 1.5 * 2.0**23
 
 FLOPS = 2 * P * D_MODEL * N_OUT
@@ -49,8 +48,8 @@ def tile_multiheadselfattention_pa_k_kernel(tc, x, W_words, W_scales, out_0, out
         psum_t = ctx.enter_context(tc.psum_pool(name="psum_t", bufs=2))
         psum_acc = ctx.enter_context(tc.psum_pool(name="psum_acc", bufs=1))
 
-        w_words = keep.tile([P, MAIN_PASSES, 2 * N_OUT], U8, align_bytes=64)
-        w_tail = [keep.tile([P, TAIL_PASSES, 2 * SECTION], U8, align_bytes=64, name="w_tail%d" % s) for s in range(3)]
+        w_qk = keep.tile([P, PASSES, 4 * SECTION], U8, align_bytes=64)
+        w_v = keep.tile([P, PASSES, 2 * SECTION], U8, align_bytes=64)
         w_scales = keep.tile([P, PASSES, N_OUT], U8, align_bytes=64)
         x_codes = keep.tile([P, PASSES, P], U32, align_bytes=64)
         x_scales = keep.tile([P, PASSES, P], U8, align_bytes=64)
@@ -98,7 +97,7 @@ def tile_multiheadselfattention_pa_k_kernel(tc, x, W_words, W_scales, out_0, out
 
         held_for = slice(0, 8 - SCALE_DMAS_AHEAD) if SCALE_DMAS_AHEAD >= 4 else slice(32, 32 + 4 - SCALE_DMAS_AHEAD)
         nc.vector.tensor_copy(
-            out=w_words[held_for, 0, 0:4].bitcast(I32), in_=w_scales[held_for, PASSES - 1, 0:4].bitcast(I32)
+            out=w_qk[held_for, 0, 0:4].bitcast(I32), in_=w_scales[held_for, PASSES - 1, 0:4].bitcast(I32)
         )
 
         partition_index = keep.tile([P, 1], I32)
@@ -136,20 +135,13 @@ def tile_multiheadselfattention_pa_k_kernel(tc, x, W_words, W_scales, out_0, out
         neg_sin = keep.tile([P, PAIRS], F32)
         nc.vector.tensor_scalar_mul(out=neg_sin[:], in0=cos_sin[:, 1, :], scalar1=-1.0)
 
-        for g in range(MAIN_PASSES):
-            nc.sync.dma_start(out=w_words[:, g, :].bitcast(I32), in_=W_words[g].bitcast(I32))
         word_rows = W_words.bitcast(I32).rearrange("g p n -> p g n")
-        for section in range(3):
-            starts = list(range(0, TAIL_PASSES, TAIL_DMA_PASSES))
-            if section == 2:
-                starts.append(TAIL_PASSES - 1)
-            for t0, t1 in zip(starts, starts[1:] + [TAIL_PASSES]):
-                nc.sync.dma_start(
-                    out=w_tail[section][:, t0:t1, :].bitcast(I32),
-                    in_=word_rows[
-                        :, MAIN_PASSES + t0 : MAIN_PASSES + t1, SECTION // 2 * section : SECTION // 2 * (section + 1)
-                    ],
-                )
+        for g in range(PASSES):
+            nc.sync.dma_start(out=w_qk[:, g, :].bitcast(I32), in_=word_rows[:, g, 0:SECTION])
+        starts = list(range(0, PASSES, V_DMA_PASSES))
+        starts.append(PASSES - 1)
+        for g0, g1 in zip(starts, starts[1:] + [PASSES]):
+            nc.sync.dma_start(out=w_v[:, g0:g1, :].bitcast(I32), in_=word_rows[:, g0:g1, SECTION : SECTION * 3 // 2])
 
         def over_heads(table, planes):
             return table.unsqueeze(1).unsqueeze(1).to_broadcast([P, planes, BANK_HEADS, PAIRS])
@@ -167,16 +159,15 @@ def tile_multiheadselfattention_pa_k_kernel(tc, x, W_words, W_scales, out_0, out
                 stop=(g == PASSES - 1),
             )
 
-        for g in range(MAIN_PASSES):
-            for n in range(BANKS):
-                mx_pass(g, n, w_words[:, g, 2 * BANK * n : 2 * BANK * (n + 1)])
+        for g in range(PASSES):
+            for n in range(QK_BANKS):
+                mx_pass(g, n, w_qk[:, g, 2 * BANK * n : 2 * BANK * (n + 1)])
 
         for section, out in enumerate((out_0, out_1, out_2)):
-            for t in range(TAIL_PASSES):
-                for half in range(2):
-                    mx_pass(
-                        MAIN_PASSES + t, 2 * section + half, w_tail[section][:, t, 2 * BANK * half : 2 * BANK * (half + 1)]
-                    )
+            if section == 2:
+                for g in range(PASSES):
+                    for half in range(2):
+                        mx_pass(g, QK_BANKS + half, w_v[:, g, 2 * BANK * half : 2 * BANK * (half + 1)])
             result = keep.tile([P, HEADS, PAIRS, 2], F32, name="result%d" % section)
             for half in range(2):
                 bank = acc[2 * section + half]

import math
from contextlib import ExitStack

import concourse.mybir as mybir
from concourse.masks import make_identity

F32 = mybir.dt.float32
BF16 = mybir.dt.bfloat16
I32 = mybir.dt.int32
U32 = mybir.dt.uint32
U8 = mybir.dt.uint8
FP8X4 = mybir.dt.float8_e4m3fn_x4
FP4X4 = mybir.dt.float4_e2m1fn_x4
ALU = mybir.AluOpType
ACT = mybir.ActivationFunctionType

P = 128
PACK = 4
K_PASS = P * PACK
BATCH, POSITIONS, D_MODEL, HEADS, HEAD_DIM = 2, 64, 8192, 16, 64
PAIRS = HEAD_DIM // 2
THETA = 100000.0
SECTION = HEADS * HEAD_DIM
N_OUT = 3 * SECTION
PASSES = D_MODEL // K_PASS
BANK = 512
BANKS = N_OUT // BANK
BANK_HEADS = BANK // HEAD_DIM
X_CHUNK_PASSES = 4
ROUND_PASSES = 2
SCALE_DMA_PASSES = 8
SCALE_DMAS_AHEAD = 4
QK_BANKS = 4
V_DMA_PASSES = 2
ROUND_TO_INTEGER = 1.5 * 2.0**23

FLOPS = 2 * P * D_MODEL * N_OUT


def tile_multiheadselfattention_pa_k_kernel(tc, x, W_words, W_scales, out_0, out_1, out_2):
    nc = tc.nc
    with ExitStack() as ctx:
        ctx.enter_context(tc.manual_schedule())
        keep = ctx.enter_context(tc.tile_pool(name="keep", bufs=1))
        x_pool = ctx.enter_context(tc.tile_pool(name="x", bufs=PASSES // X_CHUNK_PASSES))
        group_pool = ctx.enter_context(tc.tile_pool(name="group", bufs=3))
        rope_pool = ctx.enter_context(tc.tile_pool(name="rope", bufs=2))
        psum_t = ctx.enter_context(tc.psum_pool(name="psum_t", bufs=2))
        psum_acc = ctx.enter_context(tc.psum_pool(name="psum_acc", bufs=1))

        w_qk = keep.tile([P, PASSES, 4 * SECTION], U8, align_bytes=64)
        w_v = keep.tile([P, PASSES, 2 * SECTION], U8, align_bytes=64)
        w_scales = keep.tile([P, PASSES, N_OUT], U8, align_bytes=64)
        x_codes = keep.tile([P, PASSES, P], U32, align_bytes=64)
        x_scales = keep.tile([P, PASSES, P], U8, align_bytes=64)
        ident = keep.tile([P, P], F32)
        make_identity(nc, ident[:])

        x_rows = x.rearrange("b l c -> l b c")
        x_cols = X_CHUNK_PASSES * K_PASS
        x_chunks = []
        for c in range(PASSES // X_CHUNK_PASSES):
            x_sb = x_pool.tile([P, x_cols], BF16)
            nc.sync.dma_start(out=x_sb[:], in_=x_rows[:, :, c * x_cols : (c + 1) * x_cols])
            x_chunks.append(x_sb)

        scale_rows = W_scales.bitcast(I32).rearrange("g q n -> q g n")
        for g0 in range(0, PASSES, SCALE_DMA_PASSES):
            g1 = g0 + SCALE_DMA_PASSES
            nc.vector.memset(w_scales[:, g0:g1, :].bitcast(I32), 0)
            for b in range(2):
                for r in range(4):
                    nc.sync.dma_start(
                        out=w_scales[32 * b + r : P : 64, g0:g1, :].bitcast(I32),
                        in_=scale_rows[4 * b + r : 16 : 8, g0:g1, :],
                    )

        for j in range(PASSES // ROUND_PASSES):
            xt = psum_t.tile([P, ROUND_PASSES, 2, P], F32)
            for gi in range(ROUND_PASSES):
                g = ROUND_PASSES * j + gi
                words = x_chunks[g // X_CHUNK_PASSES][:].bitcast(F32)
                first = (g % X_CHUNK_PASSES) * (K_PASS // 2)
                for u in range(2):
                    nc.tensor.transpose(
                        xt[:, gi, u, :], words[:, first + u : first + K_PASS // 2 : 2], ident[:]
                    )
            grouped = group_pool.tile([P, ROUND_PASSES, P, PACK], BF16, align_bytes=64)
            nc.scalar.copy(out=grouped[:].bitcast(F32), in_=xt[:].rearrange("p g u r -> p g r u"))
            g0 = ROUND_PASSES * j
            g1 = g0 + ROUND_PASSES
            nc.vector.quantize_mx(
                out=x_codes[:, g0:g1, :].rearrange("p g r -> p (g r)").bitcast(FP8X4),
                scales=x_scales[:, g0:g1, :].rearrange("p g r -> p (g r)"),
                in_=grouped[:].rearrange("p g r t -> p (g r t)"),
            )

        held_for = slice(0, 8 - SCALE_DMAS_AHEAD) if SCALE_DMAS_AHEAD >= 4 else slice(32, 32 + 4 - SCALE_DMAS_AHEAD)
        nc.vector.tensor_copy(
            out=w_qk[held_for, 0, 0:4].bitcast(I32), in_=w_scales[held_for, PASSES - 1, 0:4].bitcast(I32)
        )

        partition_index = keep.tile([P, 1], I32)
        nc.gpsimd.iota(out=partition_index[:], pattern=[[0, 1]], base=0, channel_multiplier=1)
        pair_index = keep.tile([P, PAIRS], I32)
        nc.gpsimd.iota(out=pair_index[:], pattern=[[1, PAIRS]], base=0, channel_multiplier=0)
        position_index = keep.tile([P, 1], I32)
        nc.vector.tensor_single_scalar(
            out=position_index[:], in_=partition_index[:], scalar=1, op=ALU.arith_shift_right
        )
        position = keep.tile([P, 1], F32)
        nc.vector.tensor_copy(out=position[:], in_=position_index[:])
        pair = keep.tile([P, PAIRS], F32)
        nc.vector.tensor_copy(out=pair[:], in_=pair_index[:])
        inv_freq = keep.tile([P, PAIRS], F32)
        nc.scalar.activation(out=inv_freq[:], in_=pair[:], func=ACT.Exp, scale=-math.log(THETA) / PAIRS)
        turns = keep.tile([P, 2, PAIRS], F32)
        nc.vector.tensor_scalar(
            out=turns[:, 1, :],
            in0=inv_freq[:],
            scalar1=position[:, 0:1],
            scalar2=1.0 / (2.0 * math.pi),
            op0=ALU.mult,
            op1=ALU.mult,
        )
        nc.vector.tensor_scalar_add(out=turns[:, 0, :], in0=turns[:, 1, :], scalar1=0.25)
        shifted = keep.tile([P, 2, PAIRS], F32)
        nc.vector.tensor_scalar_add(out=shifted[:], in0=turns[:], scalar1=ROUND_TO_INTEGER)
        whole = keep.tile([P, 2, PAIRS], F32)
        nc.vector.tensor_scalar_sub(out=whole[:], in0=shifted[:], scalar1=ROUND_TO_INTEGER)
        fraction = keep.tile([P, 2, PAIRS], F32)
        nc.vector.tensor_sub(out=fraction[:], in0=turns[:], in1=whole[:])
        cos_sin = keep.tile([P, 2, PAIRS], F32)
        nc.scalar.activation(out=cos_sin[:], in_=fraction[:], func=ACT.Sin, scale=2.0 * math.pi)
        neg_sin = keep.tile([P, PAIRS], F32)
        nc.vector.tensor_scalar_mul(out=neg_sin[:], in0=cos_sin[:, 1, :], scalar1=-1.0)

        word_rows = W_words.bitcast(I32).rearrange("g p n -> p g n")
        for g in range(PASSES):
            nc.sync.dma_start(out=w_qk[:, g, :].bitcast(I32), in_=word_rows[:, g, 0:SECTION])
        starts = list(range(0, PASSES, V_DMA_PASSES))
        starts.append(PASSES - 1)
        for g0, g1 in zip(starts, starts[1:] + [PASSES]):
            nc.sync.dma_start(out=w_v[:, g0:g1, :].bitcast(I32), in_=word_rows[:, g0:g1, SECTION : SECTION * 3 // 2])

        def over_heads(table, planes):
            return table.unsqueeze(1).unsqueeze(1).to_broadcast([P, planes, BANK_HEADS, PAIRS])

        acc = [psum_acc.tile([P, BANK], F32, name="acc%d" % n) for n in range(BANKS)]

        def mx_pass(g, n, words):
            nc.tensor.matmul_mx(
                out=acc[n][:],
                lhsT=x_codes[:, g, :].bitcast(FP8X4),
                lhsT_scale=x_scales[:, g, :],
                rhs=words.bitcast(FP4X4),
                rhs_scale=w_scales[:, g, BANK * n : BANK * (n + 1)],
                start=(g == 0),
                stop=(g == PASSES - 1),
            )

        for g in range(PASSES):
            for n in range(QK_BANKS):
                mx_pass(g, n, w_qk[:, g, 2 * BANK * n : 2 * BANK * (n + 1)])

        for section, out in enumerate((out_0, out_1, out_2)):
            if section == 2:
                for g in range(PASSES):
                    for half in range(2):
                        mx_pass(g, QK_BANKS + half, w_v[:, g, 2 * BANK * half : 2 * BANK * (half + 1)])
            result = keep.tile([P, HEADS, PAIRS, 2], F32, name="result%d" % section)
            for half in range(2):
                bank = acc[2 * section + half]
                heads = slice(BANK_HEADS * half, BANK_HEADS * (half + 1))
                if section == 2:
                    copy = nc.scalar.copy if half == 0 else nc.vector.tensor_copy
                    copy(
                        out=result[:, heads, :, :],
                        in_=bank[:].rearrange("p (h i e) -> p h i e", i=PAIRS, e=2),
                    )
                    queue = nc.scalar if half == 0 else nc.sync
                    for b in range(BATCH):
                        queue.dma_start(
                            out=out[b, heads, :, :].rearrange("h l d -> l h d"),
                            in_=result[b:P:BATCH, heads, :, :].rearrange("p h i e -> p h (i e)"),
                        )
                    continue
                by_plane = bank[:].rearrange("p (h i e) -> p e h i", i=PAIRS, e=2)
                with_cos = rope_pool.tile([P, 2, BANK_HEADS, PAIRS], F32)
                nc.vector.tensor_tensor(
                    out=with_cos[:], in0=by_plane, in1=over_heads(cos_sin[:, 0, :], 2), op=ALU.mult
                )
                with_sin = rope_pool.tile([P, 2, BANK_HEADS, PAIRS], F32)
                nc.vector.tensor_tensor(
                    out=with_sin[:, 0:1, :, :], in0=by_plane[:, 1:2, :, :], in1=over_heads(neg_sin[:], 1), op=ALU.mult
                )
                nc.vector.tensor_tensor(
                    out=with_sin[:, 1:2, :, :], in0=by_plane[:, 0:1, :, :], in1=over_heads(cos_sin[:, 1, :], 1), op=ALU.mult
                )
                nc.gpsimd.tensor_tensor(
                    out=result[:, heads, :, :],
                    in0=with_cos[:].rearrange("p e h i -> p h i e"),
                    in1=with_sin[:].rearrange("p e h i -> p h i e"),
                    op=ALU.add,
                )
            if section < 2:
                nc.sync.dma_start(
                    out=out.rearrange("b h l d -> l b h d"),
                    in_=result[:].rearrange("p h i e -> p h (i e)"),
                )
